import numpy as np
import ml_dtypes


def mxq(x, axis, fmt="e4m3"):
    dtype, down = {"e4m3": (ml_dtypes.float8_e4m3fn, 7), "e5m2": (ml_dtypes.float8_e5m2, 14)}[fmt]
    v = np.moveaxis(np.asarray(x, np.float32).astype(ml_dtypes.bfloat16).astype(np.float64), axis, -1)
    blocks = v.reshape(v.shape[:-1] + (-1, 32))
    amax = np.abs(blocks).max(-1, keepdims=True)
    byte = np.maximum(np.where(amax > 0, np.frexp(amax)[1] - 1 + 127, 0) - down, 1)
    scale = np.exp2(byte - 127.0)
    codes = (blocks / scale).astype(np.float32).astype(dtype).astype(np.float64)
    return np.moveaxis((codes * scale).reshape(v.shape), -1, axis)


WIDE = False


def mx_kscale(k):
    if not WIDE:
        return np.ones(k)
    levels = np.array([10, -10, 5, -5, 0])
    if k % 512:
        return np.exp2(np.random.permutation(np.resize(levels, k // 32))).repeat(32)
    a = np.empty((k // 512, 16))
    for p in range(k // 512):
        a[p, :8] = np.random.permutation(np.resize(levels, 8))
        for g in range(8):
            far = levels[np.abs(levels - a[p, g]) >= 10]
            a[p, g + 8] = far[np.random.randint(len(far))]
    return np.exp2(a.ravel()).repeat(32)


BF16 = ml_dtypes.bfloat16


def bf(x):
    return np.asarray(x, np.float32).astype(BF16)


def f64(x):
    return np.asarray(x).astype(np.float64)


B, S, D, DFF, R = 4, 128, 1024, 4096, 512


def setup_inputs():
    t, r = mx_kscale(DFF), mx_kscale(R)
    v = np.random.standard_normal((B, S, DFF)) * 1.2
    return {"h_gelu": bf(v / (1.0 + np.exp(-1.702 * v)) * t),
            "c_proj_U": bf(np.random.standard_normal((DFF, R)) * 2.0 / np.sqrt(DFF) / t[:, None]),
            "c_proj_S": bf(np.random.uniform(size=R) * r),
            "c_proj_V": bf(np.random.standard_normal((D, R)) / np.sqrt(R) / r[None, :]),
            "c_proj_bias": bf(np.random.standard_normal(D) * 0.3)}


def reference(h_gelu, c_proj_U, c_proj_S, c_proj_V, c_proj_bias):
    us = f64(c_proj_U) * f64(c_proj_S)[None, :]
    w = f64(bf(mxq(us, 1, "e4m3") @ mxq(f64(c_proj_V), 1, "e4m3").T))
    return (mxq(f64(h_gelu), 2, "e4m3") @ mxq(w, 0, "e4m3")) + f64(c_proj_bias)

@@ -1,0 +1,264 @@
+from contextlib import ExitStack
+
+import concourse.mybir as mybir
+from concourse.masks import make_identity
+
+F32 = mybir.dt.float32
+BF16 = mybir.dt.bfloat16
+U32 = mybir.dt.uint32
+U8 = mybir.dt.uint8
+FP8X4 = mybir.dt.float8_e4m3fn_x4
+W_BANK_DT = BF16
+
+P = 128
+TOK, D, DFF, R = 512, 1024, 4096, 512
+K_PASS = 512
+G = DFF // K_PASS
+HALF = 512
+N_HALVES = D // HALF
+N_STEPS = G * N_HALVES
+LAST_STEP = N_STEPS + 1
+W_COLS = 256
+FLOPS = 2 * DFF * R * D + 2 * TOK * DFF * D
+
+C_COPY_ENGINES = ("SS", "SV")
+
+
+def tile_hybridsuperlayer_pb_kernel(tc, h_gelu, c_proj_U, c_proj_S, c_proj_V, c_proj_bias, out):
+    nc = tc.nc
+    h_rows = h_gelu.flatten_outer_dims()
+    out_rows = out.flatten_outer_dims()
+
+    with ExitStack() as ctx:
+        keep = ctx.enter_context(tc.tile_pool(name="keep", bufs=1))
+        work = ctx.enter_context(tc.tile_pool(name="work", bufs=2))
+        psum = ctx.enter_context(tc.psum_pool(name="psum", bufs=1))
+        ctx.enter_context(tc.manual_schedule())
+
+        s4 = keep.tile([P, 1, 4], BF16, name="s4", tag="s4")
+        v_raw = []
+        u_raw = []
+        h_raw = []
+        for hf in range(N_HALVES):
+            v_raw.append(keep.tile([P, 4, R], BF16, name="v_raw%d" % hf, tag="v_raw%d" % hf))
+        for g in range(G):
+            u_raw.append(keep.tile([P, 4, R], BF16, name="u_raw%d" % g, tag="u_raw%d" % g))
+            h_raw.append(keep.tile([P, 4, K_PASS], BF16, name="h_raw%d" % g, tag="h_raw%d" % g))
+
+        def load_in_pieces(dst, src, pieces):
+            step = 4 // pieces
+            for a in range(pieces):
+                nc.sync.dma_start(out=dst[:, a * step : (a + 1) * step, :], in_=src[:, a * step : (a + 1) * step, :])
+
+        def load_v(hf, pieces):
+            load_in_pieces(
+                v_raw[hf], c_proj_V[hf * HALF : (hf + 1) * HALF, :].rearrange("(j m) r -> m j r", m=P), pieces
+            )
+
+        def load_u(g, pieces):
+            load_in_pieces(
+                u_raw[g], c_proj_U[g * K_PASS : (g + 1) * K_PASS, :].rearrange("(m t) r -> m t r", t=4), pieces
+            )
+
+        def load_h(g):
+            nc.sync.dma_start(
+                out=h_raw[g][:],
+                in_=h_rows[:, g * K_PASS : (g + 1) * K_PASS].rearrange("(i m) k -> m i k", m=P),
+            )
+
+        nc.sync.dma_start(out=s4[:, 0, :], in_=c_proj_S.rearrange("(p j) -> p j", j=4))
+        load_u(0, 2)
+        load_v(0, 2)
+        load_u(1, 2)
+        for g in range(G):
+            load_h(g)
+            if g + 2 < G:
+                load_u(g + 2, 1)
+        load_v(1, 1)
+        bias_bc = keep.tile([P, D], BF16, name="bias_bc", tag="bias_bc")
+        nc.sync.dma_start(out=bias_bc[:], in_=c_proj_bias.partition_broadcast(P))
+
+        ident = keep.tile([P, P], F32, name="ident", tag="ident")
+        make_identity(nc, ident[:])
+
+        warm_sb = keep.tile([P, 512], BF16, name="warm_sb", tag="warm_sb")
+        nc.vector.memset(warm_sb[:], 0.0)
+        warm_ps = psum.tile([P, HALF], F32, name="warm_ps", tag="acc0", bufs=1)
+        for w in range(3):
+            nc.tensor.matmul(warm_ps[:], lhsT=warm_sb[:, 0:P], rhs=warm_sb[:], start=True, stop=True)
+
+        u_grp = {}
+        h_grp = {}
+        v_grp = {}
+        w_grp = {}
+        h_perm = {}
+        u_codes = {}
+        u_scales = {}
+        h_codes = {}
+        h_scales = {}
+        v_codes = {}
+        v_scales = {}
+        w_codes = {}
+        w_scales = {}
+        acc = {}
+
+        def copy_on(eng, dst, src):
+            if eng == "S":
+                nc.scalar.copy(out=dst, in_=src)
+            else:
+                nc.vector.tensor_copy(out=dst, in_=src)
+
+        def transpose_bank(word_view):
+            bank = psum.tile([P, 512], F32, name="t_bank", tag="rot", bufs=4)
+            for u in range(2):
+                for x in range(2):
+                    q = 2 * u + x
+                    nc.tensor.transpose(bank[:, q * P : (q + 1) * P], word_view(u, x), ident[:])
+            return bank
+
+        def every_2nd_word(raw, a):
+            return lambda u, x: raw[:, 2 * a + x, :].bitcast(F32)[:, u : R // 2 : 2]
+
+        def words_out(eng, grp, a, bank):
+            copy_on(
+                eng,
+                grp[:, a * 1024 : (a + 1) * 1024].bitcast(F32).rearrange("p (q u) -> p q u", u=2),
+                bank[:].rearrange("p (u q) -> p q u", u=2),
+            )
+
+        def quantize(grp, name):
+            codes = keep.tile([P, 512], U32, name=name + "_codes", tag=name + "_codes", align_bytes=64)
+            scales = keep.tile([P, 512], U8, name=name + "_scales", tag=name + "_scales", align_bytes=64)
+            nc.vector.quantize_mx(out=codes[:].bitcast(FP8X4), scales=scales[:], in_=grp[:])
+            return codes, scales
+
+        def turn_v(hf):
+            v_grp[hf] = work.tile([P, 2048], BF16, name="v_grp", tag="v_grp", bufs=1, align_bytes=64)
+            for a in range(2):
+                bank = transpose_bank(every_2nd_word(v_raw[hf], a))
+                words_out("S", v_grp[hf], a, bank)
+
+        def turn_u(g):
+            u_grp[g] = work.tile([P, 2048], BF16, name="u_grp", tag="u_grp", bufs=2, align_bytes=64)
+            for a in range(2):
+                bank = transpose_bank(every_2nd_word(u_raw[g], a))
+                nc.vector.tensor_tensor(
+                    out=u_grp[g][:, a * 1024 : (a + 1) * 1024].rearrange("p (q u e) -> p q u e", u=2, e=2),
+                    in0=bank[:].bitcast(BF16).rearrange("p (u q e) -> p q u e", u=2, e=2),
+                    in1=s4[:].rearrange("p o (u e) -> p o u e", u=2).to_broadcast([P, 256, 2, 2]),
+                    op=mybir.AluOpType.mult,
+                )
+
+        def permute_h(g):
+            h_perm[g] = work.tile([P, 2, 4, P], F32, name="h_perm", tag="h_perm", bufs=2)
+            nc.vector.tensor_copy(
+                out=h_perm[g][:], in_=h_raw[g][:].bitcast(F32).rearrange("m i (p u) -> m u i p", u=2)
+            )
+
+        def turn_h(g):
+            h_grp[g] = work.tile([P, 2048], BF16, name="h_grp", tag="h_grp", bufs=2, align_bytes=64)
+            for a in range(2):
+                bank = transpose_bank(lambda u, x: h_perm[g][:, u, 2 * a + x, :])
+                words_out("S", h_grp[g], a, bank)
+
+        def stage1(c, j):
+            hf, g = divmod(c, G)
+            if j == 0:
+                w_grp[c] = work.tile([P, 2048], BF16, name="w_grp", tag="w_grp", bufs=3, align_bytes=64)
+            bank = psum.tile([P, 4, W_COLS], W_BANK_DT, name="w_bank", tag="rot", bufs=4)
+            for t in range(4):
+                nc.tensor.matmul_mx(
+                    out=bank[:, t, :],
+                    lhsT=u_codes[g][:, t * P : (t + 1) * P].bitcast(FP8X4),
+                    lhsT_scale=u_scales[g][:, t * P : (t + 1) * P],
+                    rhs=v_codes[hf][:, j * W_COLS : (j + 1) * W_COLS].bitcast(FP8X4),
+                    rhs_scale=v_scales[hf][:, j * W_COLS : (j + 1) * W_COLS],
+                    start=True,
+                    stop=True,
+                )
+            copy_on(
+                C_COPY_ENGINES[hf][j],
+                w_grp[c][:, j * 4 * W_COLS : (j + 1) * 4 * W_COLS].rearrange("p (n t) -> p n t", t=4),
+                bank[:].rearrange("p t n -> p n t"),
+            )
+
+        def quantize_w(c):
+            w_codes[c] = work.tile([P, 512], U32, name="w_codes", tag="w_codes", bufs=5, align_bytes=64)
+            w_scales[c] = work.tile([P, 512], U8, name="w_scales", tag="w_scales", bufs=5, align_bytes=64)
+            nc.vector.quantize_mx(out=w_codes[c][:].bitcast(FP8X4), scales=w_scales[c][:], in_=w_grp[c][:])
+
+        def stage2(c, i):
+            hf, g = divmod(c, G)
+            if g == 0:
+                acc[i] = psum.tile([P, HALF], F32, name="acc%d" % i, tag="acc%d" % i, bufs=1)
+            nc.tensor.matmul_mx(
+                out=acc[i][:],
+                lhsT=h_codes[g][:, i * P : (i + 1) * P].bitcast(FP8X4),
+                lhsT_scale=h_scales[g][:, i * P : (i + 1) * P],
+                rhs=w_codes[c][:].bitcast(FP8X4),
+                rhs_scale=w_scales[c][:],
+                start=(g == 0),
+                stop=(g == G - 1),
+            )
+            if g == G - 1:
+                o_sb = work.tile([P, HALF], F32, name="o_sb", tag="o_sb", bufs=4)
+                nc.vector.tensor_tensor(
+                    out=o_sb[:],
+                    in0=acc[i][:],
+                    in1=bias_bc[:, hf * HALF : (hf + 1) * HALF],
+                    op=mybir.AluOpType.add,
+                )
+                nc.sync.dma_start(
+                    out=out_rows[i * P : (i + 1) * P, hf * HALF : (hf + 1) * HALF], in_=o_sb[:]
+                )
+
+        def d_plan(k):
+            if 0 <= k - 2 < G:
+                return [(k - 2, i) for i in range(4)]
+            if G <= k - 3 < N_STEPS - 2:
+                return [(k - 3, i) for i in range(4)]
+            if k == LAST_STEP:
+                return [(c, i) for i in range(4) for c in (N_STEPS - 2, N_STEPS - 1)]
+            return []
+
+        def mx_run(k, part):
+            plan = d_plan(k)
+            half = len(plan) // 2
+            mine = plan[part * half : (part + 1) * half]
+            if mine:
+                stage2(mine[0][0], mine[0][1])
+            if 0 <= k + 1 < N_STEPS:
+                stage1(k + 1, part)
+            for c, i in mine[1:]:
+                stage2(c, i)
+
+        for k in range(-2, LAST_STEP + 1):
+            if 0 <= k - 1 < G:
+                h_codes[k - 1], h_scales[k - 1] = quantize(h_grp[k - 1], "h%d" % (k - 1))
+            if k == -2:
+                turn_u(0)
+                turn_v(0)
+                u_codes[0], u_scales[0] = quantize(u_grp[0], "u0")
+                v_codes[0] = keep.tile([P, 512], U32, name="v0_codes", tag="v0_codes", align_bytes=64)
+                v_scales[0] = keep.tile([P, 512], U8, name="v0_scales", tag="v0_scales", align_bytes=64)
+                for a in range(2):
+                    nc.vector.quantize_mx(
+                        out=v_codes[0][:, a * 256 : (a + 1) * 256].bitcast(FP8X4),
+                        scales=v_scales[0][:, a * 256 : (a + 1) * 256],
+                        in_=v_grp[0][:, a * 1024 : (a + 1) * 1024],
+                    )
+            elif k == G - 2:
+                turn_v(1)
+                v_codes[1], v_scales[1] = quantize(v_grp[1], "v1")
+            elif k + 2 < G:
+                turn_u(k + 2)
+            if 0 <= k < N_STEPS:
+                quantize_w(k)
+            mx_run(k, 0)
+            if -2 < k and k + 2 < G:
+                u_codes[k + 2], u_scales[k + 2] = quantize(u_grp[k + 2], "u%d" % (k + 2))
+            if 0 <= k + 1 < G:
+                permute_h(k + 1)
+            if 0 <= k < G:
+                turn_h(k)
+            mx_run(k, 1)

@@ -21,7 +21,7 @@ LAST_STEP = N_STEPS + 1
 W_COLS = 256
 FLOPS = 2 * DFF * R * D + 2 * TOK * DFF * D
 
-C_COPY_ENGINES = ("SS", "SV")
+W_ON_VECTOR = (8, 9, 11, 13)
 
 
 def tile_hybridsuperlayer_pb_kernel(tc, h_gelu, c_proj_U, c_proj_S, c_proj_V, c_proj_bias, out):
@@ -177,7 +177,7 @@ def tile_hybridsuperlayer_pb_kernel(tc, h_gelu, c_proj_U, c_proj_S, c_proj_V, c_
                     stop=True,
                 )
             copy_on(
-                C_COPY_ENGINES[hf][j],
+                "V" if (j == 1 and c in W_ON_VECTOR) else "S",
                 w_grp[c][:, j * 4 * W_COLS : (j + 1) * 4 * W_COLS].rearrange("p (n t) -> p n t", t=4),
                 bank[:].rearrange("p t n -> p n t"),
             )

@@ -84,8 +84,12 @@ def tile_hybridsuperlayer_pb_kernel(tc, h_gelu, c_proj_U, c_proj_S, c_proj_V, c_
         warm_sb = keep.tile([P, 512], BF16, name="warm_sb", tag="warm_sb")
         nc.vector.memset(warm_sb[:], 0.0)
         warm_ps = psum.tile([P, HALF], F32, name="warm_ps", tag="acc0", bufs=1)
-        for w in range(3):
-            nc.tensor.matmul(warm_ps[:], lhsT=warm_sb[:, 0:P], rhs=warm_sb[:], start=True, stop=True)
+
+        def warm(n):
+            for w in range(n):
+                nc.tensor.matmul(warm_ps[:], lhsT=warm_sb[:, 0:P], rhs=warm_sb[:], start=True, stop=True)
+
+        warm(6)
 
         u_grp = {}
         h_grp = {}
@@ -237,7 +241,9 @@ def tile_hybridsuperlayer_pb_kernel(tc, h_gelu, c_proj_U, c_proj_S, c_proj_V, c_
                 h_codes[k - 1], h_scales[k - 1] = quantize(h_grp[k - 1], "h%d" % (k - 1))
             if k == -2:
                 turn_u(0)
+                warm(2)
                 turn_v(0)
+                warm(2)
                 u_codes[0], u_scales[0] = quantize(u_grp[0], "u0")
                 v_codes[0] = keep.tile([P, 512], U32, name="v0_codes", tag="v0_codes", align_bytes=64)
                 v_scales[0] = keep.tile([P, 512], U8, name="v0_scales", tag="v0_scales", align_bytes=64)

@@ -22,6 +22,7 @@ W_COLS = 256
 FLOPS = 2 * DFF * R * D + 2 * TOK * DFF * D
 
 W_ON_VECTOR = (8, 9, 11, 13)
+EARLY_BANKS = ("rot", "rot", "rot", "rot", "acc1", "acc2", "acc3")
 
 
 def tile_hybridsuperlayer_pb_kernel(tc, h_gelu, c_proj_U, c_proj_S, c_proj_V, c_proj_bias, out):
@@ -112,8 +113,17 @@ def tile_hybridsuperlayer_pb_kernel(tc, h_gelu, c_proj_U, c_proj_S, c_proj_V, c_
             else:
                 nc.vector.tensor_copy(out=dst, in_=src)
 
+        banks_given = []
+
+        def next_bank(shape, dtype, name):
+            tag = "rot"
+            if not acc:
+                tag = EARLY_BANKS[len(banks_given) % len(EARLY_BANKS)]
+            banks_given.append(tag)
+            return psum.tile(shape, dtype, name=name, tag=tag, bufs=4 if tag == "rot" else 1)
+
         def transpose_bank(word_view):
-            bank = psum.tile([P, 512], F32, name="t_bank", tag="rot", bufs=4)
+            bank = next_bank([P, 512], F32, "t_bank")
             for u in range(2):
                 for x in range(2):
                     q = 2 * u + x
@@ -169,7 +179,7 @@ def tile_hybridsuperlayer_pb_kernel(tc, h_gelu, c_proj_U, c_proj_S, c_proj_V, c_
             hf, g = divmod(c, G)
             if j == 0:
                 w_grp[c] = work.tile([P, 2048], BF16, name="w_grp", tag="w_grp", bufs=3, align_bytes=64)
-            bank = psum.tile([P, 4, W_COLS], W_BANK_DT, name="w_bank", tag="rot", bufs=4)
+            bank = next_bank([P, 4, W_COLS], W_BANK_DT, "w_bank")
             for t in range(4):
                 nc.tensor.matmul_mx(
                     out=bank[:, t, :],

@@ -67,7 +67,7 @@ def tile_hybridsuperlayer_pb_kernel(tc, h_gelu, c_proj_U, c_proj_S, c_proj_V, c_
                 in_=h_rows[:, g * K_PASS : (g + 1) * K_PASS].rearrange("(i m) k -> m i k", m=P),
             )
 
-        nc.sync.dma_start(out=s4[:, 0, :], in_=c_proj_S.rearrange("(p j) -> p j", j=4))
+        nc.scalar.dma_start(out=s4[:, 0, :], in_=c_proj_S.rearrange("(p j) -> p j", j=4))
         load_u(0, 2)
         load_v(0, 2)
         load_u(1, 2)

@@ -18,10 +18,14 @@ HALF = 512
 N_HALVES = D // HALF
 N_STEPS = G * N_HALVES
 LAST_STEP = N_STEPS + 1
+S1_DOUBLE = N_STEPS - 3
 W_COLS = 256
 FLOPS = 2 * DFF * R * D + 2 * TOK * DFF * D
 
-W_ON_VECTOR = (8, 9, 11, 13)
+W_ON_VECTOR = (8, 9, 11, 13, 14, 15)
+LAST_TILE = 3
+TAIL_STEPS = 3
+PIECE = 256
 EARLY_BANKS = ("rot", "rot", "rot", "rot", "acc1", "acc2", "acc3")
 
 
@@ -106,6 +110,8 @@ def tile_hybridsuperlayer_pb_kernel(tc, h_gelu, c_proj_U, c_proj_S, c_proj_V, c_
         w_codes = {}
         w_scales = {}
         acc = {}
+        early_sum = {}
+        piece = {}
 
         def copy_on(eng, dst, src):
             if eng == "S":
@@ -197,12 +203,14 @@ def tile_hybridsuperlayer_pb_kernel(tc, h_gelu, c_proj_U, c_proj_S, c_proj_V, c_
             )
 
         def quantize_w(c):
-            w_codes[c] = work.tile([P, 512], U32, name="w_codes", tag="w_codes", bufs=5, align_bytes=64)
-            w_scales[c] = work.tile([P, 512], U8, name="w_scales", tag="w_scales", bufs=5, align_bytes=64)
+            w_codes[c] = work.tile([P, 512], U32, name="w_codes", tag="w_codes", bufs=6, align_bytes=64)
+            w_scales[c] = work.tile([P, 512], U8, name="w_scales", tag="w_scales", bufs=6, align_bytes=64)
             nc.vector.quantize_mx(out=w_codes[c][:].bitcast(FP8X4), scales=w_scales[c][:], in_=w_grp[c][:])
 
         def stage2(c, i):
             hf, g = divmod(c, G)
+            in_pieces = hf == N_HALVES - 1 and i == LAST_TILE
+            closes_at = G - 1 - TAIL_STEPS if in_pieces else G - 1
             if g == 0:
                 acc[i] = psum.tile([P, HALF], F32, name="acc%d" % i, tag="acc%d" % i, bufs=1)
             nc.tensor.matmul_mx(
@@ -212,9 +220,9 @@ def tile_hybridsuperlayer_pb_kernel(tc, h_gelu, c_proj_U, c_proj_S, c_proj_V, c_
                 rhs=w_codes[c][:].bitcast(FP8X4),
                 rhs_scale=w_scales[c][:],
                 start=(g == 0),
-                stop=(g == G - 1),
+                stop=(g == closes_at),
             )
-            if g == G - 1:
+            if g == closes_at:
                 o_sb = work.tile([P, HALF], F32, name="o_sb", tag="o_sb", bufs=4)
                 nc.vector.tensor_tensor(
                     out=o_sb[:],
@@ -222,29 +230,76 @@ def tile_hybridsuperlayer_pb_kernel(tc, h_gelu, c_proj_U, c_proj_S, c_proj_V, c_
                     in1=bias_bc[:, hf * HALF : (hf + 1) * HALF],
                     op=mybir.AluOpType.add,
                 )
-                nc.sync.dma_start(
-                    out=out_rows[i * P : (i + 1) * P, hf * HALF : (hf + 1) * HALF], in_=o_sb[:]
+                if in_pieces:
+                    early_sum[0] = o_sb
+                else:
+                    nc.sync.dma_start(
+                        out=out_rows[i * P : (i + 1) * P, hf * HALF : (hf + 1) * HALF], in_=o_sb[:]
+                    )
+
+        def stage2_piece(c, q):
+            hf, g = divmod(c, G)
+            i = LAST_TILE
+            cols = slice(q * PIECE, (q + 1) * PIECE)
+            if g == G - TAIL_STEPS:
+                piece[q] = next_bank([P, PIECE], F32, "piece")
+            nc.tensor.matmul_mx(
+                out=piece[q][:],
+                lhsT=h_codes[g][:, i * P : (i + 1) * P].bitcast(FP8X4),
+                lhsT_scale=h_scales[g][:, i * P : (i + 1) * P],
+                rhs=w_codes[c][:, cols].bitcast(FP8X4),
+                rhs_scale=w_scales[c][:, cols],
+                start=(g == G - TAIL_STEPS),
+                stop=(g == G - 1),
+            )
+            if g == G - 1:
+                o_fin = work.tile([P, PIECE], F32, name="o_fin", tag="o_fin", bufs=2)
+                nc.vector.tensor_tensor(
+                    out=o_fin[:], in0=piece[q][:], in1=early_sum[0][:, cols], op=mybir.AluOpType.add
                 )
+                nc.sync.dma_start(
+                    out=out_rows[i * P : (i + 1) * P, hf * HALF + q * PIECE : hf * HALF + (q + 1) * PIECE],
+                    in_=o_fin[:],
+                )
+
+        def one_pass(c, i):
+            if i < 0:
+                stage2_piece(c, -1 - i)
+            else:
+                stage2(c, i)
 
         def d_plan(k):
             if 0 <= k - 2 < G:
                 return [(k - 2, i) for i in range(4)]
-            if G <= k - 3 < N_STEPS - 2:
+            if G <= k - 3 < S1_DOUBLE - 3:
+                return [(k - 3, i) for i in range(4)]
+            if k == S1_DOUBLE + 1:
+                return [(c, i) for c in (k - 4, k - 3) for i in range(4)]
+            if k == S1_DOUBLE + 2:
                 return [(k - 3, i) for i in range(4)]
             if k == LAST_STEP:
-                return [(c, i) for i in range(4) for c in (N_STEPS - 2, N_STEPS - 1)]
+                last = range(N_STEPS - TAIL_STEPS, N_STEPS)
+                whole = [(c, i) for i in range(LAST_TILE) for c in last]
+                return whole + [(c, -1 - q) for q in range(HALF // PIECE) for c in last]
+            return []
+
+        def c_plan(k, part):
+            if k == S1_DOUBLE:
+                return [(k + 1 + part, 0), (k + 1 + part, 1)]
+            if 0 <= k + 1 < N_STEPS - 1 and k < S1_DOUBLE:
+                return [(k + 1, part)]
             return []
 
         def mx_run(k, part):
             plan = d_plan(k)
             half = len(plan) // 2
-            mine = plan[part * half : (part + 1) * half]
+            mine = plan[half:] if part else plan[:half]
             if mine:
-                stage2(mine[0][0], mine[0][1])
-            if 0 <= k + 1 < N_STEPS:
-                stage1(k + 1, part)
+                one_pass(mine[0][0], mine[0][1])
+            for c, j in c_plan(k, part):
+                stage1(c, j)
             for c, i in mine[1:]:
-                stage2(c, i)
+                one_pass(c, i)
 
         for k in range(-2, LAST_STEP + 1):
             if 0 <= k - 1 < G:

@@ -323,12 +323,17 @@ def tile_hybridsuperlayer_pb_kernel(tc, h_gelu, c_proj_U, c_proj_S, c_proj_V, c_
                 v_codes[1], v_scales[1] = quantize(v_grp[1], "v1")
             elif k + 2 < G:
                 turn_u(k + 2)
-            if 0 <= k < N_STEPS:
+            w_last = k in (0, 1)
+            if 0 <= k < N_STEPS and not w_last:
                 quantize_w(k)
             mx_run(k, 0)
+            if w_last:
+                permute_h(k + 1)
             if -2 < k and k + 2 < G:
                 u_codes[k + 2], u_scales[k + 2] = quantize(u_grp[k + 2], "u%d" % (k + 2))
-            if 0 <= k + 1 < G:
+            if w_last:
+                quantize_w(k)
+            elif 0 <= k + 1 < G:
                 permute_h(k + 1)
             if 0 <= k < G:
                 turn_h(k)

@@ -26,6 +26,7 @@ W_ON_VECTOR = (8, 9, 11, 13, 14, 15)
 LAST_TILE = 3
 TAIL_STEPS = 3
 PIECE = 256
+SHIFT = 64
 EARLY_BANKS = ("rot", "rot", "rot", "rot", "acc1", "acc2", "acc3")
 
 
@@ -147,9 +148,10 @@ def tile_hybridsuperlayer_pb_kernel(tc, h_gelu, c_proj_U, c_proj_S, c_proj_V, c_
             )
 
         def quantize(grp, name):
-            codes = keep.tile([P, 512], U32, name=name + "_codes", tag=name + "_codes", align_bytes=64)
-            scales = keep.tile([P, 512], U8, name=name + "_scales", tag=name + "_scales", align_bytes=64)
-            nc.vector.quantize_mx(out=codes[:].bitcast(FP8X4), scales=scales[:], in_=grp[:])
+            codes = keep.tile([P, 512], U32, name=name + "_codes", tag=name + "_codes", align_bytes=256)
+            plane = keep.tile([P, SHIFT + 512], U8, name=name + "_scales", tag=name + "_scales", align_bytes=256)
+            scales = plane[:, SHIFT : SHIFT + 512]
+            nc.vector.quantize_mx(out=codes[:].bitcast(FP8X4), scales=scales, in_=grp[:])
             return codes, scales
 
         def turn_v(hf):
@@ -203,9 +205,10 @@ def tile_hybridsuperlayer_pb_kernel(tc, h_gelu, c_proj_U, c_proj_S, c_proj_V, c_
             )
 
         def quantize_w(c):
-            w_codes[c] = work.tile([P, 512], U32, name="w_codes", tag="w_codes", bufs=6, align_bytes=64)
-            w_scales[c] = work.tile([P, 512], U8, name="w_scales", tag="w_scales", bufs=6, align_bytes=64)
-            nc.vector.quantize_mx(out=w_codes[c][:].bitcast(FP8X4), scales=w_scales[c][:], in_=w_grp[c][:])
+            w_codes[c] = work.tile([P, 512], U32, name="w_codes", tag="w_codes", bufs=6, align_bytes=256)
+            w_plane = work.tile([P, SHIFT + 512], U8, name="w_scales", tag="w_scales", bufs=6, align_bytes=256)
+            w_scales[c] = w_plane[:, SHIFT : SHIFT + 512]
+            nc.vector.quantize_mx(out=w_codes[c][:].bitcast(FP8X4), scales=w_scales[c], in_=w_grp[c][:])
 
         def stage2(c, i):
             hf, g = divmod(c, G)
@@ -218,7 +221,7 @@ def tile_hybridsuperlayer_pb_kernel(tc, h_gelu, c_proj_U, c_proj_S, c_proj_V, c_
                 lhsT=h_codes[g][:, i * P : (i + 1) * P].bitcast(FP8X4),
                 lhsT_scale=h_scales[g][:, i * P : (i + 1) * P],
                 rhs=w_codes[c][:].bitcast(FP8X4),
-                rhs_scale=w_scales[c][:],
+                rhs_scale=w_scales[c],
                 start=(g == 0),
                 stop=(g == closes_at),
             )
@@ -310,8 +313,9 @@ def tile_hybridsuperlayer_pb_kernel(tc, h_gelu, c_proj_U, c_proj_S, c_proj_V, c_
                 turn_v(0)
                 warm(2)
                 u_codes[0], u_scales[0] = quantize(u_grp[0], "u0")
-                v_codes[0] = keep.tile([P, 512], U32, name="v0_codes", tag="v0_codes", align_bytes=64)
-                v_scales[0] = keep.tile([P, 512], U8, name="v0_scales", tag="v0_scales", align_bytes=64)
+                v_codes[0] = keep.tile([P, 512], U32, name="v0_codes", tag="v0_codes", align_bytes=256)
+                v0_plane = keep.tile([P, SHIFT + 512], U8, name="v0_scales", tag="v0_scales", align_bytes=256)
+                v_scales[0] = v0_plane[:, SHIFT : SHIFT + 512]
                 for a in range(2):
                     nc.vector.quantize_mx(
                         out=v_codes[0][:, a * 256 : (a + 1) * 256].bitcast(FP8X4),

from contextlib import ExitStack

import concourse.mybir as mybir
from concourse.masks import make_identity

F32 = mybir.dt.float32
BF16 = mybir.dt.bfloat16
U32 = mybir.dt.uint32
U8 = mybir.dt.uint8
FP8X4 = mybir.dt.float8_e4m3fn_x4
W_BANK_DT = BF16

P = 128
TOK, D, DFF, R = 512, 1024, 4096, 512
K_PASS = 512
G = DFF // K_PASS
HALF = 512
N_HALVES = D // HALF
N_STEPS = G * N_HALVES
LAST_STEP = N_STEPS + 1
S1_DOUBLE = N_STEPS - 3
W_COLS = 256
FLOPS = 2 * DFF * R * D + 2 * TOK * DFF * D

W_ON_VECTOR = (8, 9, 11, 13, 14, 15)
LAST_TILE = 3
TAIL_STEPS = 3
PIECE = 256
SHIFT = 64
EARLY_BANKS = ("rot", "rot", "rot", "rot", "acc1", "acc2", "acc3")


def tile_hybridsuperlayer_pb_kernel(tc, h_gelu, c_proj_U, c_proj_S, c_proj_V, c_proj_bias, out):
    nc = tc.nc
    h_rows = h_gelu.flatten_outer_dims()
    out_rows = out.flatten_outer_dims()

    with ExitStack() as ctx:
        keep = ctx.enter_context(tc.tile_pool(name="keep", bufs=1))
        work = ctx.enter_context(tc.tile_pool(name="work", bufs=2))
        psum = ctx.enter_context(tc.psum_pool(name="psum", bufs=1))
        ctx.enter_context(tc.manual_schedule())

        s4 = keep.tile([P, 1, 4], BF16, name="s4", tag="s4")
        v_raw = []
        u_raw = []
        h_raw = []
        for hf in range(N_HALVES):
            v_raw.append(keep.tile([P, 4, R], BF16, name="v_raw%d" % hf, tag="v_raw%d" % hf))
        for g in range(G):
            u_raw.append(keep.tile([P, 4, R], BF16, name="u_raw%d" % g, tag="u_raw%d" % g))
            h_raw.append(keep.tile([P, 4, K_PASS], BF16, name="h_raw%d" % g, tag="h_raw%d" % g))

        def load_in_pieces(dst, src, pieces):
            step = 4 // pieces
            for a in range(pieces):
                nc.sync.dma_start(out=dst[:, a * step : (a + 1) * step, :], in_=src[:, a * step : (a + 1) * step, :])

        def load_v(hf, pieces):
            load_in_pieces(
                v_raw[hf], c_proj_V[hf * HALF : (hf + 1) * HALF, :].rearrange("(j m) r -> m j r", m=P), pieces
            )

        def load_u(g, pieces):
            load_in_pieces(
                u_raw[g], c_proj_U[g * K_PASS : (g + 1) * K_PASS, :].rearrange("(m t) r -> m t r", t=4), pieces
            )

        def load_h(g):
            nc.sync.dma_start(
                out=h_raw[g][:],
                in_=h_rows[:, g * K_PASS : (g + 1) * K_PASS].rearrange("(i m) k -> m i k", m=P),
            )

        nc.scalar.dma_start(out=s4[:, 0, :], in_=c_proj_S.rearrange("(p j) -> p j", j=4))
        load_u(0, 2)
        load_v(0, 2)
        load_u(1, 2)
        for g in range(G):
            load_h(g)
            if g + 2 < G:
                load_u(g + 2, 1)
        load_v(1, 1)
        bias_bc = keep.tile([P, D], BF16, name="bias_bc", tag="bias_bc")
        nc.sync.dma_start(out=bias_bc[:], in_=c_proj_bias.partition_broadcast(P))

        ident = keep.tile([P, P], F32, name="ident", tag="ident")
        make_identity(nc, ident[:])

        warm_sb = keep.tile([P, 512], BF16, name="warm_sb", tag="warm_sb")
        nc.vector.memset(warm_sb[:], 0.0)
        warm_ps = psum.tile([P, HALF], F32, name="warm_ps", tag="acc0", bufs=1)

        def warm(n):
            for w in range(n):
                nc.tensor.matmul(warm_ps[:], lhsT=warm_sb[:, 0:P], rhs=warm_sb[:], start=True, stop=True)

        warm(6)

        u_grp = {}
        h_grp = {}
        v_grp = {}
        w_grp = {}
        h_perm = {}
        u_codes = {}
        u_scales = {}
        h_codes = {}
        h_scales = {}
        v_codes = {}
        v_scales = {}
        w_codes = {}
        w_scales = {}
        acc = {}
        early_sum = {}
        piece = {}

        def copy_on(eng, dst, src):
            if eng == "S":
                nc.scalar.copy(out=dst, in_=src)
            else:
                nc.vector.tensor_copy(out=dst, in_=src)

        banks_given = []

        def next_bank(shape, dtype, name):
            tag = "rot"
            if not acc:
                tag = EARLY_BANKS[len(banks_given) % len(EARLY_BANKS)]
            banks_given.append(tag)
            return psum.tile(shape, dtype, name=name, tag=tag, bufs=4 if tag == "rot" else 1)

        def transpose_bank(word_view):
            bank = next_bank([P, 512], F32, "t_bank")
            for u in range(2):
                for x in range(2):
                    q = 2 * u + x
                    nc.tensor.transpose(bank[:, q * P : (q + 1) * P], word_view(u, x), ident[:])
            return bank

        def every_2nd_word(raw, a):
            return lambda u, x: raw[:, 2 * a + x, :].bitcast(F32)[:, u : R // 2 : 2]

        def words_out(eng, grp, a, bank):
            copy_on(
                eng,
                grp[:, a * 1024 : (a + 1) * 1024].bitcast(F32).rearrange("p (q u) -> p q u", u=2),
                bank[:].rearrange("p (u q) -> p q u", u=2),
            )

        def quantize(grp, name):
            codes = keep.tile([P, 512], U32, name=name + "_codes", tag=name + "_codes", align_bytes=256)
            plane = keep.tile([P, SHIFT + 512], U8, name=name + "_scales", tag=name + "_scales", align_bytes=256)
            scales = plane[:, SHIFT : SHIFT + 512]
            nc.vector.quantize_mx(out=codes[:].bitcast(FP8X4), scales=scales, in_=grp[:])
            return codes, scales

        def turn_v(hf):
            v_grp[hf] = work.tile([P, 2048], BF16, name="v_grp", tag="v_grp", bufs=1, align_bytes=64)
            for a in range(2):
                bank = transpose_bank(every_2nd_word(v_raw[hf], a))
                words_out("S", v_grp[hf], a, bank)

        def turn_u(g):
            u_grp[g] = work.tile([P, 2048], BF16, name="u_grp", tag="u_grp", bufs=2, align_bytes=64)
            for a in range(2):
                bank = transpose_bank(every_2nd_word(u_raw[g], a))
                nc.vector.tensor_tensor(
                    out=u_grp[g][:, a * 1024 : (a + 1) * 1024].rearrange("p (q u e) -> p q u e", u=2, e=2),
                    in0=bank[:].bitcast(BF16).rearrange("p (u q e) -> p q u e", u=2, e=2),
                    in1=s4[:].rearrange("p o (u e) -> p o u e", u=2).to_broadcast([P, 256, 2, 2]),
                    op=mybir.AluOpType.mult,
                )

        def permute_h(g):
            h_perm[g] = work.tile([P, 2, 4, P], F32, name="h_perm", tag="h_perm", bufs=2)
            nc.vector.tensor_copy(
                out=h_perm[g][:], in_=h_raw[g][:].bitcast(F32).rearrange("m i (p u) -> m u i p", u=2)
            )

        def turn_h(g):
            h_grp[g] = work.tile([P, 2048], BF16, name="h_grp", tag="h_grp", bufs=2, align_bytes=64)
            for a in range(2):
                bank = transpose_bank(lambda u, x: h_perm[g][:, u, 2 * a + x, :])
                words_out("S", h_grp[g], a, bank)

        def stage1(c, j):
            hf, g = divmod(c, G)
            if j == 0:
                w_grp[c] = work.tile([P, 2048], BF16, name="w_grp", tag="w_grp", bufs=3, align_bytes=64)
            bank = next_bank([P, 4, W_COLS], W_BANK_DT, "w_bank")
            for t in range(4):
                nc.tensor.matmul_mx(
                    out=bank[:, t, :],
                    lhsT=u_codes[g][:, t * P : (t + 1) * P].bitcast(FP8X4),
                    lhsT_scale=u_scales[g][:, t * P : (t + 1) * P],
                    rhs=v_codes[hf][:, j * W_COLS : (j + 1) * W_COLS].bitcast(FP8X4),
                    rhs_scale=v_scales[hf][:, j * W_COLS : (j + 1) * W_COLS],
                    start=True,
                    stop=True,
                )
            copy_on(
                "V" if (j == 1 and c in W_ON_VECTOR) else "S",
                w_grp[c][:, j * 4 * W_COLS : (j + 1) * 4 * W_COLS].rearrange("p (n t) -> p n t", t=4),
                bank[:].rearrange("p t n -> p n t"),
            )

        def quantize_w(c):
            w_codes[c] = work.tile([P, 512], U32, name="w_codes", tag="w_codes", bufs=6, align_bytes=256)
            w_plane = work.tile([P, SHIFT + 512], U8, name="w_scales", tag="w_scales", bufs=6, align_bytes=256)
            w_scales[c] = w_plane[:, SHIFT : SHIFT + 512]
            nc.vector.quantize_mx(out=w_codes[c][:].bitcast(FP8X4), scales=w_scales[c], in_=w_grp[c][:])

        def stage2(c, i):
            hf, g = divmod(c, G)
            in_pieces = hf == N_HALVES - 1 and i == LAST_TILE
            closes_at = G - 1 - TAIL_STEPS if in_pieces else G - 1
            if g == 0:
                acc[i] = psum.tile([P, HALF], F32, name="acc%d" % i, tag="acc%d" % i, bufs=1)
            nc.tensor.matmul_mx(
                out=acc[i][:],
                lhsT=h_codes[g][:, i * P : (i + 1) * P].bitcast(FP8X4),
                lhsT_scale=h_scales[g][:, i * P : (i + 1) * P],
                rhs=w_codes[c][:].bitcast(FP8X4),
                rhs_scale=w_scales[c],
                start=(g == 0),
                stop=(g == closes_at),
            )
            if g == closes_at:
                o_sb = work.tile([P, HALF], F32, name="o_sb", tag="o_sb", bufs=4)
                nc.vector.tensor_tensor(
                    out=o_sb[:],
                    in0=acc[i][:],
                    in1=bias_bc[:, hf * HALF : (hf + 1) * HALF],
                    op=mybir.AluOpType.add,
                )
                if in_pieces:
                    early_sum[0] = o_sb
                else:
                    nc.sync.dma_start(
                        out=out_rows[i * P : (i + 1) * P, hf * HALF : (hf + 1) * HALF], in_=o_sb[:]
                    )

        def stage2_piece(c, q):
            hf, g = divmod(c, G)
            i = LAST_TILE
            cols = slice(q * PIECE, (q + 1) * PIECE)
            if g == G - TAIL_STEPS:
                piece[q] = next_bank([P, PIECE], F32, "piece")
            nc.tensor.matmul_mx(
                out=piece[q][:],
                lhsT=h_codes[g][:, i * P : (i + 1) * P].bitcast(FP8X4),
                lhsT_scale=h_scales[g][:, i * P : (i + 1) * P],
                rhs=w_codes[c][:, cols].bitcast(FP8X4),
                rhs_scale=w_scales[c][:, cols],
                start=(g == G - TAIL_STEPS),
                stop=(g == G - 1),
            )
            if g == G - 1:
                o_fin = work.tile([P, PIECE], F32, name="o_fin", tag="o_fin", bufs=2)
                nc.vector.tensor_tensor(
                    out=o_fin[:], in0=piece[q][:], in1=early_sum[0][:, cols], op=mybir.AluOpType.add
                )
                nc.sync.dma_start(
                    out=out_rows[i * P : (i + 1) * P, hf * HALF + q * PIECE : hf * HALF + (q + 1) * PIECE],
                    in_=o_fin[:],
                )

        def one_pass(c, i):
            if i < 0:
                stage2_piece(c, -1 - i)
            else:
                stage2(c, i)

        def d_plan(k):
            if 0 <= k - 2 < G:
                return [(k - 2, i) for i in range(4)]
            if G <= k - 3 < S1_DOUBLE - 3:
                return [(k - 3, i) for i in range(4)]
            if k == S1_DOUBLE + 1:
                return [(c, i) for c in (k - 4, k - 3) for i in range(4)]
            if k == S1_DOUBLE + 2:
                return [(k - 3, i) for i in range(4)]
            if k == LAST_STEP:
                last = range(N_STEPS - TAIL_STEPS, N_STEPS)
                whole = [(c, i) for i in range(LAST_TILE) for c in last]
                return whole + [(c, -1 - q) for q in range(HALF // PIECE) for c in last]
            return []

        def c_plan(k, part):
            if k == S1_DOUBLE:
                return [(k + 1 + part, 0), (k + 1 + part, 1)]
            if 0 <= k + 1 < N_STEPS - 1 and k < S1_DOUBLE:
                return [(k + 1, part)]
            return []

        def mx_run(k, part):
            plan = d_plan(k)
            half = len(plan) // 2
            mine = plan[half:] if part else plan[:half]
            if mine:
                one_pass(mine[0][0], mine[0][1])
            for c, j in c_plan(k, part):
                stage1(c, j)
            for c, i in mine[1:]:
                one_pass(c, i)

        for k in range(-2, LAST_STEP + 1):
            if 0 <= k - 1 < G:
                h_codes[k - 1], h_scales[k - 1] = quantize(h_grp[k - 1], "h%d" % (k - 1))
            if k == -2:
                turn_u(0)
                warm(2)
                turn_v(0)
                warm(2)
                u_codes[0], u_scales[0] = quantize(u_grp[0], "u0")
                v_codes[0] = keep.tile([P, 512], U32, name="v0_codes", tag="v0_codes", align_bytes=256)
                v0_plane = keep.tile([P, SHIFT + 512], U8, name="v0_scales", tag="v0_scales", align_bytes=256)
                v_scales[0] = v0_plane[:, SHIFT : SHIFT + 512]
                for a in range(2):
                    nc.vector.quantize_mx(
                        out=v_codes[0][:, a * 256 : (a + 1) * 256].bitcast(FP8X4),
                        scales=v_scales[0][:, a * 256 : (a + 1) * 256],
                        in_=v_grp[0][:, a * 1024 : (a + 1) * 1024],
                    )
            elif k == G - 2:
                turn_v(1)
                v_codes[1], v_scales[1] = quantize(v_grp[1], "v1")
            elif k + 2 < G:
                turn_u(k + 2)
            w_last = k in (0, 1)
            if 0 <= k < N_STEPS and not w_last:
                quantize_w(k)
            mx_run(k, 0)
            if w_last:
                permute_h(k + 1)
            if -2 < k and k + 2 < G:
                u_codes[k + 2], u_scales[k + 2] = quantize(u_grp[k + 2], "u%d" % (k + 2))
            if w_last:
                quantize_w(k)
            elif 0 <= k + 1 < G:
                permute_h(k + 1)
            if 0 <= k < G:
                turn_h(k)
            mx_run(k, 1)
